import numpy as np
import ml_dtypes


def mxq(x, axis, fmt="e4m3"):
    dtype, down = {"e4m3": (ml_dtypes.float8_e4m3fn, 7), "e5m2": (ml_dtypes.float8_e5m2, 14)}[fmt]
    v = np.moveaxis(np.asarray(x, np.float32).astype(ml_dtypes.bfloat16).astype(np.float64), axis, -1)
    blocks = v.reshape(v.shape[:-1] + (-1, 32))
    amax = np.abs(blocks).max(-1, keepdims=True)
    byte = np.maximum(np.where(amax > 0, np.frexp(amax)[1] - 1 + 127, 0) - down, 1)
    scale = np.exp2(byte - 127.0)
    codes = (blocks / scale).astype(np.float32).astype(dtype).astype(np.float64)
    return np.moveaxis((codes * scale).reshape(v.shape), -1, axis)


WIDE = False


def mx_kscale(k):
    if not WIDE:
        return np.ones(k)
    levels = np.array([10, -10, 5, -5, 0])
    a = np.random.permutation(np.resize(levels, k // 512 * 4)).reshape(k // 512, 4)
    idx = np.arange(k)
    return np.exp2(a[idx // 512, idx % 128 // 32])


BF16 = ml_dtypes.bfloat16


def bf(x):
    return np.asarray(x, np.float32).astype(BF16)


def f64(x):
    return np.asarray(x).astype(np.float64)


B, N, C_IN, C_OUT, RANK = 2, 2048, 1024, 1024, 128


def sigmoid(v):
    return 1.0 / (1.0 + np.exp(-v))


def setup_inputs():
    s = mx_kscale(C_IN)
    return {"x": bf(np.random.standard_normal((B, N, C_IN)) * s),
            "freq": bf(np.random.standard_normal((B, RANK * (C_IN + C_OUT)))),
            "phase_shift": bf(np.random.standard_normal((B, 2 * C_OUT))),
            "weight": bf(np.random.standard_normal((C_OUT, C_IN)) / np.sqrt(C_IN) / s[None, :])}


def reference(x, freq, phase_shift, weight):
    x, freq, phase_shift, weight = f64(x), f64(freq), f64(phase_shift), f64(weight)
    c_out, c_in = weight.shape
    rank = freq.shape[1] // (c_in + c_out)
    left = freq[:, :c_out * rank].reshape(-1, c_out, rank)
    right = freq[:, c_out * rank:].reshape(-1, rank, c_in)
    modulation = (left @ right) / np.sqrt(rank)
    modulation = sigmoid(modulation) - 0.5
    W = weight[None, :, :] * (modulation + 1.0)
    out = mxq(x, 2, "e4m3") @ mxq(W, 2, "e4m3").transpose(0, 2, 1)
    freq_shift = phase_shift[:, :c_out][:, None, :]
    phase = ((phase_shift[:, c_out:] - 30.0) / 15.0)[:, None, :]
    return np.sin(freq_shift * out + phase)

@@ -1,0 +1,292 @@
+import math
+from contextlib import ExitStack
+
+import concourse.mybir as mybir
+from concourse.masks import make_identity
+
+F32 = mybir.dt.float32
+BF16 = mybir.dt.bfloat16
+I32 = mybir.dt.int32
+U32 = mybir.dt.uint32
+U8 = mybir.dt.uint8
+FP8X4 = mybir.dt.float8_e4m3fn_x4
+ACT = mybir.ActivationFunctionType
+ALU = mybir.AluOpType
+
+P = 128
+B, N, CI, CO, R = 2, 2048, 1024, 1024, 128
+FLOPS = 2 * B * N * CI * CO + 2 * B * CO * CI * R
+ROWS = N // P
+TQ = 4
+NCH = B * (ROWS // TQ)
+NPAIR = NCH * 4
+TWO_PI = 2.0 * math.pi
+X_LEAD = 6
+
+
+def tile_fmmlayer_t_kernel(tc, x, freq, phase_shift, weight, out):
+    nc = tc.nc
+    with ExitStack() as ctx:
+        keep = ctx.enter_context(tc.tile_pool(name="keep", bufs=1))
+        xs_pool = ctx.enter_context(tc.tile_pool(name="xs", bufs=4))
+        st2 = ctx.enter_context(tc.tile_pool(name="st2", bufs=2))
+        st3 = ctx.enter_context(tc.tile_pool(name="st3", bufs=3))
+        psum = ctx.enter_context(tc.psum_pool(name="psum", bufs=2))
+
+        ident_b = keep.tile([P, P], BF16, name="ident_b")
+        make_identity(nc, ident_b[:])
+        ident_f = keep.tile([P, P], F32, name="ident_f")
+        make_identity(nc, ident_f[:])
+        warm_in = keep.tile([P, 1], F32, name="warm_in")
+        nc.vector.memset(warm_in[:], 0.0)
+        warm_out = keep.tile([P, 1], F32, name="warm_out")
+        nc.scalar.activation(out=warm_out[:], in_=warm_in[:], func=ACT.Silu)
+
+        psz = keep.tile([P, P], BF16, name="psz")
+        nc.vector.memset(psz[:], 0.0)
+        nc.sync.dma_start(out=psz[0:32, :], in_=phase_shift.rearrange("b (r c) -> (b r) c", c=P))
+        lf = []
+        rt = []
+        for b in range(B):
+            lf.append(keep.tile([P, 8, R], BF16, name="lf%d" % b))
+            rt.append(keep.tile([P, CI], BF16, name="rt%d" % b))
+
+        def load_freq(b):
+            nc.sync.dma_start(out=lf[b][:], in_=freq[b, 0 : CO * R].rearrange("(t p r) -> p t r", t=8, p=P))
+            nc.sync.dma_start(out=rt[b][:], in_=freq[b, CO * R : CO * R + R * CI].rearrange("(r i) -> r i", r=R))
+
+        load_freq(0)
+        wview = weight.rearrange("(t p) i -> p t i", p=P)
+        wn = []
+        for k in range(4):
+            wn.append(keep.tile([P, 2, CI], BF16, name="wn%d" % k))
+            nc.sync.dma_start(out=wn[k][:], in_=wview[:, 2 * k : 2 * k + 2, :])
+
+        xs = {}
+
+        def load_x(c):
+            b, q = divmod(c, 4)
+            xs_t = xs_pool.tile([P, TQ, CI], BF16, name="xs_t", tag="xs")
+            nc.sync.dma_start(
+                out=xs_t[:], in_=x[b].rearrange("(j s) i -> j s i", s=ROWS)[:, TQ * q : TQ * q + TQ, :]
+            )
+            xs[c] = xs_t
+
+        load_x(0)
+        load_freq(1)
+        load_x(1)
+        load_x(2)
+        load_x(3)
+
+        pps = psum.tile([P, P], BF16, name="pps", tag="a")
+        nc.tensor.transpose(pps[:], psz[:], ident_b[:])
+        psv = pps[:, 0:32].rearrange("p (b h o) -> p b h o", b=B, h=2)
+        fs2 = keep.tile([P, B, 8], F32, name="fs2")
+        ph2 = keep.tile([P, B, 8], F32, name="ph2")
+        nc.vector.tensor_scalar(out=fs2[:], in0=psv[:, :, 0, :], scalar1=1.0 / TWO_PI, scalar2=None, op0=ALU.mult)
+        nc.vector.tensor_scalar(
+            out=ph2[:], in0=psv[:, :, 1, :], scalar1=-30.0, scalar2=1.0 / (15.0 * TWO_PI), op0=ALU.add, op1=ALU.mult
+        )
+
+        lT = []
+        for b in range(B):
+            lT.append(keep.tile([P, CO], BF16, name="lT%d" % b))
+
+        def left_t(b):
+            plf = psum.tile([P, 8, P], BF16, name="plf", tag="a")
+            for t in range(8):
+                nc.tensor.transpose(plf[:, t, :], lf[b][:, t, :], ident_b[:])
+            nc.scalar.copy(out=lT[b][:], in_=plf[:].rearrange("p t o -> p (t o)"))
+
+        wTh = keep.tile([P, 2, CO, 4], BF16, name="wTh")
+        wThf = wTh[:].bitcast(F32)
+
+        def weight_t(k):
+            flat = wn[k][:].rearrange("p t i -> p (t i)")
+            nc.vector.tensor_scalar(out=flat, in0=flat, scalar1=0.5, scalar2=None, op0=ALU.mult)
+            wnf = wn[k][:].bitcast(F32)
+            for g in range(2):
+                pw = psum.tile([P, 2, 256], F32, name="pw", tag="a")
+                for u in range(2):
+                    for ol in range(2):
+                        c0 = 256 * g + 128 * u
+                        nc.tensor.transpose(pw[:, u, ol * P : (ol + 1) * P], wnf[:, ol, c0 : c0 + P], ident_f[:])
+                nc.scalar.copy(out=wThf[:, g, 256 * k : 256 * k + 256, :], in_=pw[:].rearrange("p u o -> p o u"))
+
+        wc = []
+        wsc = []
+        for b in range(B):
+            wc.append(keep.tile([P, 2, CO], U32, name="wc%d" % b, align_bytes=64))
+            wsc.append(keep.tile([P, 2, CO], U8, name="wsc%d" % b, align_bytes=64))
+
+        def w_unit(b, g, oq):
+            rtv = rt[b][:].rearrange("r (g u p e) -> r g u e p", g=2, u=2, p=P, e=2)
+            th = st2.tile([P, 256, 4], F32, name="th", tag="th")
+            for ol in range(2):
+                ot = 2 * oq + ol
+                pm = psum.tile([P, 4, P], F32, name="pm", tag="a")
+                for u in range(2):
+                    for e in range(2):
+                        nc.tensor.matmul(
+                            out=pm[:, 2 * u + e, :],
+                            lhsT=rtv[:, g, u, e, :],
+                            rhs=lT[b][:, ot * P : (ot + 1) * P],
+                            start=True,
+                            stop=True,
+                        )
+                nc.scalar.activation(
+                    out=th[:, ol * P : (ol + 1) * P, :],
+                    in_=pm[:].rearrange("p t o -> p o t"),
+                    func=ACT.Tanh,
+                    scale=0.5 / math.sqrt(R),
+                )
+            gw = st2.tile([P, 256, 4], BF16, name="gw", tag="gw", align_bytes=64)
+            nc.vector.scalar_tensor_tensor(
+                out=gw[:].rearrange("p o t -> p (o t)"),
+                in0=th[:].rearrange("p o t -> p (o t)"),
+                scalar=2.0,
+                in1=wTh[:, g, 256 * oq : 256 * oq + 256, :].rearrange("p o t -> p (o t)"),
+                op0=ALU.add,
+                op1=ALU.mult,
+            )
+            nc.vector.quantize_mx(
+                out=wc[b][:, g, 256 * oq : 256 * oq + 256].bitcast(FP8X4),
+                scales=wsc[b][:, g, 256 * oq : 256 * oq + 256],
+                in_=gw[:].rearrange("p o t -> p (o t)"),
+            )
+
+        xc = {}
+        xsc = {}
+        gx = {}
+
+        def x_sub(s):
+            c, sub = divmod(s, 4)
+            g, tp = divmod(sub, 2)
+            if sub == 0:
+                xc_t = st3.tile([P, 2, 512], U32, name="xc_t", tag="xc", align_bytes=64)
+                xsc_t = st3.tile([P, 2, 512], U8, name="xsc_t", tag="xsc", align_bytes=64)
+                xc[c] = xc_t
+                xsc[c] = xsc_t
+            if tp == 0:
+                gx_t = st3.tile([P, 512, 4], BF16, name="gx_t", tag="gx", align_bytes=64)
+                gx[(c, g)] = gx_t
+            xf = xs[c][:].bitcast(F32)
+            px = psum.tile([P, 2, 256], F32, name="px", tag="x")
+            for u in range(2):
+                for tl in range(2):
+                    c0 = 256 * g + 128 * u
+                    nc.tensor.transpose(px[:, u, tl * P : (tl + 1) * P], xf[:, 2 * tp + tl, c0 : c0 + P], ident_f[:])
+            dst = gx[(c, g)][:].bitcast(F32)[:, 256 * tp : 256 * tp + 256, :]
+            src = px[:].rearrange("p u n -> p n u")
+            if sub == 0:
+                nc.scalar.copy(out=dst, in_=src)
+            else:
+                nc.vector.tensor_copy(out=dst, in_=src)
+            if sub == 3 and c + 4 < NCH:
+                load_x(c + 4)
+
+        def x_quant(c, g):
+            nc.vector.quantize_mx(
+                out=xc[c][:, g, :].bitcast(FP8X4),
+                scales=xsc[c][:, g, :],
+                in_=gx[(c, g)][:].rearrange("p n t -> p (n t)"),
+            )
+
+        def x_step(s):
+            if s < 4 * NCH:
+                x_sub(s)
+            if s >= 2 and s % 2 == 0 and s - 2 < 4 * NCH:
+                c, sub = divmod(s - 2, 4)
+                x_quant(c, sub // 2)
+
+        ys = {}
+        us = {}
+        obs = {}
+
+        def s12(i):
+            c, pr = divmod(i, 4)
+            b = c // 4
+            u_t = st3.tile([P, 2, 512], F32, name="u_t", tag="u")
+            us[i] = u_t
+            for ol in range(2):
+                ot = 2 * pr + ol
+                py = psum.tile([P, 512], F32, name="py", tag="y")
+                for g in range(2):
+                    nc.tensor.matmul_mx(
+                        out=py[:],
+                        lhsT=wc[b][:, g, ot * P : (ot + 1) * P].bitcast(FP8X4),
+                        lhsT_scale=wsc[b][:, g, ot * P : (ot + 1) * P],
+                        rhs=xc[c][:, g, :].bitcast(FP8X4),
+                        rhs_scale=xsc[c][:, g, :],
+                        start=(g == 0),
+                        stop=(g == 1),
+                    )
+                ys[(i, ol)] = py
+            for ol in range(2):
+                ot = 2 * pr + ol
+                nc.scalar.activation(
+                    out=u_t[:, ol, :],
+                    in_=ys[(i, ol)][:],
+                    func=ACT.Identity,
+                    scale=fs2[:, b, ot : ot + 1],
+                    bias=ph2[:, b, ot : ot + 1],
+                )
+
+        def s345(i):
+            c, pr = divmod(i, 4)
+            b, q = divmod(c, 4)
+            u_t = us[i]
+            k_t = st2.tile([P, 2, 512], I32, name="k_t", tag="k")
+            nc.vector.tensor_copy(out=k_t[:], in_=u_t[:])
+            r_t = st3.tile([P, 2, 512], F32, name="r_t", tag="r")
+            nc.vector.tensor_tensor(out=r_t[:], in0=u_t[:], in1=k_t[:], op=ALU.subtract)
+            if pr == 0:
+                ob_t = st2.tile([P, TQ, CO], F32, name="ob_t", tag="ob")
+                obs[c] = ob_t
+            pts = []
+            for ol in range(2):
+                pt = psum.tile([P, TQ, P], F32, name="pt", tag="t")
+                for t in range(TQ):
+                    nc.tensor.transpose(pt[:, t, :], r_t[:, ol, t * P : (t + 1) * P], ident_f[:])
+                pts.append(pt)
+            for ol in range(2):
+                ot = 2 * pr + ol
+                nc.scalar.activation(
+                    out=obs[c][:, :, ot * P : (ot + 1) * P], in_=pts[ol][:], func=ACT.Sin, scale=TWO_PI
+                )
+            if pr % 2 == 1:
+                h = pr // 2
+                nc.sync.dma_start(
+                    out=out[b].rearrange("(j s) o -> j s o", s=ROWS)[:, TQ * q : TQ * q + TQ, 512 * h : 512 * h + 512],
+                    in_=obs[c][:, :, 512 * h : 512 * h + 512],
+                )
+
+        left_t(0)
+        weight_t(0)
+        w_unit(0, 0, 0)
+        w_unit(0, 1, 0)
+        x_step(0)
+        x_step(1)
+        weight_t(1)
+        w_unit(0, 0, 1)
+        w_unit(0, 1, 1)
+        x_step(2)
+        x_step(3)
+        weight_t(2)
+        w_unit(0, 0, 2)
+        w_unit(0, 1, 2)
+        x_step(4)
+        weight_t(3)
+        w_unit(0, 0, 3)
+        w_unit(0, 1, 3)
+        x_step(5)
+        left_t(1)
+        for i in range(NPAIR + 1):
+            if i < NPAIR:
+                s12(i)
+            if i >= 1:
+                s345(i - 1)
+            x_step(i + X_LEAD)
+            if i < 16 and i % 2 == 0:
+                w = i // 2
+                w_unit(1, w % 2, w // 2)

@@ -21,7 +21,18 @@ TQ = 4
 NCH = B * (ROWS // TQ)
 NPAIR = NCH * 4
 TWO_PI = 2.0 * math.pi
-X_LEAD = 6
+
+HEAD = 8
+HEAD_TAGS = ("a", "a", "y", "y", "t", "t")
+D_K, D_R, D_T = 1, 2, 3
+X_LEAD = 7
+U_DVE_FROM = 24
+
+
+def take(queue):
+    items = list(queue)
+    queue[:] = []
+    return items
 
 
 def tile_fmmlayer_t_kernel(tc, x, freq, phase_shift, weight, out):
@@ -31,7 +42,9 @@ def tile_fmmlayer_t_kernel(tc, x, freq, phase_shift, weight, out):
         xs_pool = ctx.enter_context(tc.tile_pool(name="xs", bufs=4))
         st2 = ctx.enter_context(tc.tile_pool(name="st2", bufs=2))
         st3 = ctx.enter_context(tc.tile_pool(name="st3", bufs=3))
+        st4 = ctx.enter_context(tc.tile_pool(name="st4", bufs=4))
         psum = ctx.enter_context(tc.psum_pool(name="psum", bufs=2))
+        ctx.enter_context(tc.manual_schedule())
 
         ident_b = keep.tile([P, P], BF16, name="ident_b")
         make_identity(nc, ident_b[:])
@@ -47,19 +60,19 @@ def tile_fmmlayer_t_kernel(tc, x, freq, phase_shift, weight, out):
         nc.sync.dma_start(out=psz[0:32, :], in_=phase_shift.rearrange("b (r c) -> (b r) c", c=P))
         lf = []
         rt = []
+        wn = []
         for b in range(B):
             lf.append(keep.tile([P, 8, R], BF16, name="lf%d" % b))
             rt.append(keep.tile([P, CI], BF16, name="rt%d" % b))
+        for k in range(4):
+            wn.append(keep.tile([P, 2, CI], BF16, name="wn%d" % k))
+        wview = weight.rearrange("(t p) i -> p t i", p=P)
 
         def load_freq(b):
             nc.sync.dma_start(out=lf[b][:], in_=freq[b, 0 : CO * R].rearrange("(t p r) -> p t r", t=8, p=P))
             nc.sync.dma_start(out=rt[b][:], in_=freq[b, CO * R : CO * R + R * CI].rearrange("(r i) -> r i", r=R))
 
-        load_freq(0)
-        wview = weight.rearrange("(t p) i -> p t i", p=P)
-        wn = []
-        for k in range(4):
-            wn.append(keep.tile([P, 2, CI], BF16, name="wn%d" % k))
+        def load_w(k):
             nc.sync.dma_start(out=wn[k][:], in_=wview[:, 2 * k : 2 * k + 2, :])
 
         xs = {}
@@ -72,13 +85,31 @@ def tile_fmmlayer_t_kernel(tc, x, freq, phase_shift, weight, out):
             )
             xs[c] = xs_t
 
+        load_freq(0)
+        load_w(0)
         load_x(0)
+        load_w(1)
+        load_w(2)
+        load_w(3)
         load_freq(1)
         load_x(1)
         load_x(2)
         load_x(3)
 
-        pps = psum.tile([P, P], BF16, name="pps", tag="a")
+        later_act = []
+        later_dve = []
+        pending = []
+        head = {"on": False, "n": 0}
+
+        def w_bank(shape, dtype):
+            tag = "a"
+            if head["on"]:
+                tag = HEAD_TAGS[head["n"] % len(HEAD_TAGS)]
+                head["n"] += 1
+            wb = psum.tile(shape, dtype, name="wb", tag=tag)
+            return wb
+
+        pps = w_bank([P, P], BF16)
         nc.tensor.transpose(pps[:], psz[:], ident_b[:])
         psv = pps[:, 0:32].rearrange("p (b h o) -> p b h o", b=B, h=2)
         fs2 = keep.tile([P, B, 8], F32, name="fs2")
@@ -89,77 +120,136 @@ def tile_fmmlayer_t_kernel(tc, x, freq, phase_shift, weight, out):
         )
 
         lT = []
-        for b in range(B):
-            lT.append(keep.tile([P, CO], BF16, name="lT%d" % b))
-
-        def left_t(b):
-            plf = psum.tile([P, 8, P], BF16, name="plf", tag="a")
-            for t in range(8):
-                nc.tensor.transpose(plf[:, t, :], lf[b][:, t, :], ident_b[:])
-            nc.scalar.copy(out=lT[b][:], in_=plf[:].rearrange("p t o -> p (t o)"))
-
-        wTh = keep.tile([P, 2, CO, 4], BF16, name="wTh")
-        wThf = wTh[:].bitcast(F32)
-
-        def weight_t(k):
-            flat = wn[k][:].rearrange("p t i -> p (t i)")
-            nc.vector.tensor_scalar(out=flat, in0=flat, scalar1=0.5, scalar2=None, op0=ALU.mult)
-            wnf = wn[k][:].bitcast(F32)
-            for g in range(2):
-                pw = psum.tile([P, 2, 256], F32, name="pw", tag="a")
-                for u in range(2):
-                    for ol in range(2):
-                        c0 = 256 * g + 128 * u
-                        nc.tensor.transpose(pw[:, u, ol * P : (ol + 1) * P], wnf[:, ol, c0 : c0 + P], ident_f[:])
-                nc.scalar.copy(out=wThf[:, g, 256 * k : 256 * k + 256, :], in_=pw[:].rearrange("p u o -> p o u"))
-
         wc = []
         wsc = []
         for b in range(B):
+            lT.append(keep.tile([P, CO], BF16, name="lT%d" % b))
             wc.append(keep.tile([P, 2, CO], U32, name="wc%d" % b, align_bytes=64))
             wsc.append(keep.tile([P, 2, CO], U8, name="wsc%d" % b, align_bytes=64))
+        wTh = keep.tile([P, 2, CO, 4], BF16, name="wTh")
+        wThf = wTh[:].bitcast(F32)
 
-        def w_unit(b, g, oq):
+        def step_left(b):
+            plf = w_bank([P, 8, P], BF16)
+            for t in range(8):
+                nc.tensor.transpose(plf[:, t, :], lf[b][:, t, :], ident_b[:])
+            later_act.append(lambda: nc.scalar.copy(out=lT[b][:], in_=plf[:].rearrange("p t o -> p (t o)")))
+
+        def step_halve(k):
+            flat = wn[k][:].rearrange("p t i -> p (t i)")
+            nc.vector.tensor_scalar(out=flat, in0=flat, scalar1=0.5, scalar2=None, op0=ALU.mult)
+
+        def step_wt(k, g):
+            wnf = wn[k][:].bitcast(F32)
+            pw = w_bank([P, 2, 256], F32)
+            for u in range(2):
+                for ol in range(2):
+                    c0 = 256 * g + 128 * u
+                    nc.tensor.transpose(pw[:, u, ol * P : (ol + 1) * P], wnf[:, ol, c0 : c0 + P], ident_f[:])
+            dst = wThf[:, g, 256 * k : 256 * k + 256, :]
+            src = pw[:].rearrange("p u o -> p o u")
+            if g == 0:
+                later_act.append(lambda: nc.scalar.copy(out=dst, in_=src))
+            else:
+                later_dve.append(lambda: nc.vector.tensor_copy(out=dst, in_=src))
+
+        th_now = {}
+
+        def step_w(b, g, oq, ol):
+            if ol == 0:
+                th_new = st3.tile([P, 256, 4], F32, name="th_new", tag="th")
+                th_now["t"] = th_new
+            th = th_now["t"]
+            ot = 2 * oq + ol
             rtv = rt[b][:].rearrange("r (g u p e) -> r g u e p", g=2, u=2, p=P, e=2)
-            th = st2.tile([P, 256, 4], F32, name="th", tag="th")
-            for ol in range(2):
-                ot = 2 * oq + ol
-                pm = psum.tile([P, 4, P], F32, name="pm", tag="a")
-                for u in range(2):
-                    for e in range(2):
-                        nc.tensor.matmul(
-                            out=pm[:, 2 * u + e, :],
-                            lhsT=rtv[:, g, u, e, :],
-                            rhs=lT[b][:, ot * P : (ot + 1) * P],
-                            start=True,
-                            stop=True,
-                        )
+            pm = w_bank([P, 4, P], F32)
+            for u in range(2):
+                for e in range(2):
+                    nc.tensor.matmul(
+                        out=pm[:, 2 * u + e, :],
+                        lhsT=rtv[:, g, u, e, :],
+                        rhs=lT[b][:, ot * P : (ot + 1) * P],
+                        start=True,
+                        stop=True,
+                    )
+
+            def quant(gw):
+                nc.vector.quantize_mx(
+                    out=wc[b][:, g, 256 * oq : 256 * oq + 256].bitcast(FP8X4),
+                    scales=wsc[b][:, g, 256 * oq : 256 * oq + 256],
+                    in_=gw[:].rearrange("p o t -> p (o t)"),
+                )
+
+            def modulate():
+                gw = st2.tile([P, 256, 4], BF16, name="gw", tag="gw", align_bytes=64)
+                nc.vector.scalar_tensor_tensor(
+                    out=gw[:].rearrange("p o t -> p (o t)"),
+                    in0=th[:].rearrange("p o t -> p (o t)"),
+                    scalar=2.0,
+                    in1=wTh[:, g, 256 * oq : 256 * oq + 256, :].rearrange("p o t -> p (o t)"),
+                    op0=ALU.add,
+                    op1=ALU.mult,
+                )
+                pending.append(lambda: quant(gw))
+
+            def tanh():
                 nc.scalar.activation(
                     out=th[:, ol * P : (ol + 1) * P, :],
                     in_=pm[:].rearrange("p t o -> p o t"),
                     func=ACT.Tanh,
                     scale=0.5 / math.sqrt(R),
                 )
-            gw = st2.tile([P, 256, 4], BF16, name="gw", tag="gw", align_bytes=64)
-            nc.vector.scalar_tensor_tensor(
-                out=gw[:].rearrange("p o t -> p (o t)"),
-                in0=th[:].rearrange("p o t -> p (o t)"),
-                scalar=2.0,
-                in1=wTh[:, g, 256 * oq : 256 * oq + 256, :].rearrange("p o t -> p (o t)"),
-                op0=ALU.add,
-                op1=ALU.mult,
-            )
-            nc.vector.quantize_mx(
-                out=wc[b][:, g, 256 * oq : 256 * oq + 256].bitcast(FP8X4),
-                scales=wsc[b][:, g, 256 * oq : 256 * oq + 256],
-                in_=gw[:].rearrange("p o t -> p (o t)"),
-            )
+                if ol == 1:
+                    pending.append(modulate)
+
+            later_act.append(tanh)
+
+        w_steps = []
+
+        def add_w(b, oq):
+            for g in range(2):
+                for ol in range(2):
+                    w_steps.append((True, lambda g=g, ol=ol: step_w(b, g, oq, ol)))
+
+        def add_wt(k):
+            for g in range(2):
+                w_steps.append((True, lambda g=g: step_wt(k, g)))
+
+        w_steps.append((False, lambda: step_halve(0)))
+        w_steps.append((True, lambda: step_left(0)))
+        for k in range(4):
+            add_wt(k)
+            if k < 3:
+                w_steps.append((False, lambda k=k: step_halve(k + 1)))
+            add_w(0, k)
+        w_steps.append((True, lambda: step_left(1)))
+        for k in range(4):
+            add_w(1, k)
+        w_pos = {"i": 0}
+
+        def w_free():
+            while w_pos["i"] < len(w_steps) and not w_steps[w_pos["i"]][0]:
+                w_steps[w_pos["i"]][1]()
+                w_pos["i"] += 1
+
+        def w_next():
+            w_free()
+            w_steps[w_pos["i"]][1]()
+            w_pos["i"] += 1
+            w_free()
 
         xc = {}
         xsc = {}
         gx = {}
 
-        def x_sub(s):
+        def x_quant(c, g):
+            nc.vector.quantize_mx(
+                out=xc[c][:, g, :].bitcast(FP8X4),
+                scales=xsc[c][:, g, :],
+                in_=gx[(c, g)][:].rearrange("p n t -> p (n t)"),
+            )
+
+        def step_x(s):
             c, sub = divmod(s, 4)
             g, tp = divmod(sub, 2)
             if sub == 0:
@@ -168,7 +258,7 @@ def tile_fmmlayer_t_kernel(tc, x, freq, phase_shift, weight, out):
                 xc[c] = xc_t
                 xsc[c] = xsc_t
             if tp == 0:
-                gx_t = st3.tile([P, 512, 4], BF16, name="gx_t", tag="gx", align_bytes=64)
+                gx_t = st4.tile([P, 512, 4], BF16, name="gx_t", tag="gx", align_bytes=64)
                 gx[(c, g)] = gx_t
             xf = xs[c][:].bitcast(F32)
             px = psum.tile([P, 2, 256], F32, name="px", tag="x")
@@ -178,36 +268,27 @@ def tile_fmmlayer_t_kernel(tc, x, freq, phase_shift, weight, out):
                     nc.tensor.transpose(px[:, u, tl * P : (tl + 1) * P], xf[:, 2 * tp + tl, c0 : c0 + P], ident_f[:])
             dst = gx[(c, g)][:].bitcast(F32)[:, 256 * tp : 256 * tp + 256, :]
             src = px[:].rearrange("p u n -> p n u")
-            if sub == 0:
-                nc.scalar.copy(out=dst, in_=src)
+            if s % 2 == 0:
+                later_act.append(lambda: nc.scalar.copy(out=dst, in_=src))
             else:
-                nc.vector.tensor_copy(out=dst, in_=src)
+                later_dve.append(lambda: nc.vector.tensor_copy(out=dst, in_=src))
             if sub == 3 and c + 4 < NCH:
                 load_x(c + 4)
-
-        def x_quant(c, g):
-            nc.vector.quantize_mx(
-                out=xc[c][:, g, :].bitcast(FP8X4),
-                scales=xsc[c][:, g, :],
-                in_=gx[(c, g)][:].rearrange("p n t -> p (n t)"),
-            )
-
-        def x_step(s):
-            if s < 4 * NCH:
-                x_sub(s)
-            if s >= 2 and s % 2 == 0 and s - 2 < 4 * NCH:
-                c, sub = divmod(s - 2, 4)
-                x_quant(c, sub // 2)
+            if tp == 1:
+                later_dve.append(lambda: pending.append(lambda: pending.append(lambda: x_quant(c, g))))
 
         ys = {}
         us = {}
-        obs = {}
+        ks = {}
+        rs = {}
 
-        def s12(i):
+        def where(i):
             c, pr = divmod(i, 4)
-            b = c // 4
-            u_t = st3.tile([P, 2, 512], F32, name="u_t", tag="u")
-            us[i] = u_t
+            b, q = divmod(c, 4)
+            return b, q, c, pr
+
+        def s_mx(i):
+            b, q, c, pr = where(i)
             for ol in range(2):
                 ot = 2 * pr + ol
                 py = psum.tile([P, 512], F32, name="py", tag="y")
@@ -222,71 +303,101 @@ def tile_fmmlayer_t_kernel(tc, x, freq, phase_shift, weight, out):
                         stop=(g == 1),
                     )
                 ys[(i, ol)] = py
+            u_t = st4.tile([P, 2, 512], F32, name="u_t", tag="u")
+            us[i] = u_t
+
+        def s_u(i, on_dve):
+            b, q, c, pr = where(i)
             for ol in range(2):
                 ot = 2 * pr + ol
-                nc.scalar.activation(
-                    out=u_t[:, ol, :],
-                    in_=ys[(i, ol)][:],
-                    func=ACT.Identity,
-                    scale=fs2[:, b, ot : ot + 1],
-                    bias=ph2[:, b, ot : ot + 1],
-                )
+                if (i >= U_DVE_FROM and i % 2 == 0 and ol == 1) != on_dve:
+                    continue
+                if on_dve:
+                    nc.vector.tensor_scalar(
+                        out=us[i][:, ol, :],
+                        in0=ys[(i, ol)][:],
+                        scalar1=fs2[:, b, ot : ot + 1],
+                        scalar2=ph2[:, b, ot : ot + 1],
+                        op0=ALU.mult,
+                        op1=ALU.add,
+                    )
+                else:
+                    nc.scalar.activation(
+                        out=us[i][:, ol, :],
+                        in_=ys[(i, ol)][:],
+                        func=ACT.Identity,
+                        scale=fs2[:, b, ot : ot + 1],
+                        bias=ph2[:, b, ot : ot + 1],
+                    )
 
-        def s345(i):
-            c, pr = divmod(i, 4)
-            b, q = divmod(c, 4)
-            u_t = us[i]
-            k_t = st2.tile([P, 2, 512], I32, name="k_t", tag="k")
-            nc.vector.tensor_copy(out=k_t[:], in_=u_t[:])
+        def s_k(i):
+            k_t = st3.tile([P, 2, 512], I32, name="k_t", tag="k")
+            nc.vector.tensor_copy(out=k_t[:], in_=us[i][:])
+            ks[i] = k_t
+
+        def s_r(i):
             r_t = st3.tile([P, 2, 512], F32, name="r_t", tag="r")
-            nc.vector.tensor_tensor(out=r_t[:], in0=u_t[:], in1=k_t[:], op=ALU.subtract)
-            if pr == 0:
-                ob_t = st2.tile([P, TQ, CO], F32, name="ob_t", tag="ob")
-                obs[c] = ob_t
+            nc.vector.tensor_tensor(out=r_t[:], in0=us[i][:], in1=ks[i][:], op=ALU.subtract)
+            rs[i] = r_t
+
+        def s_out(i):
+            b, q, c, pr = where(i)
             pts = []
             for ol in range(2):
                 pt = psum.tile([P, TQ, P], F32, name="pt", tag="t")
                 for t in range(TQ):
-                    nc.tensor.transpose(pt[:, t, :], r_t[:, ol, t * P : (t + 1) * P], ident_f[:])
+                    nc.tensor.transpose(pt[:, t, :], rs[i][:, ol, t * P : (t + 1) * P], ident_f[:])
                 pts.append(pt)
+            ob = st3.tile([P, TQ, 2 * P], F32, name="ob", tag="ob")
+            oview = out[b].rearrange("(j s) o -> j s o", s=ROWS)[:, TQ * q : TQ * q + TQ, :]
             for ol in range(2):
-                ot = 2 * pr + ol
-                nc.scalar.activation(
-                    out=obs[c][:, :, ot * P : (ot + 1) * P], in_=pts[ol][:], func=ACT.Sin, scale=TWO_PI
-                )
-            if pr % 2 == 1:
-                h = pr // 2
-                nc.sync.dma_start(
-                    out=out[b].rearrange("(j s) o -> j s o", s=ROWS)[:, TQ * q : TQ * q + TQ, 512 * h : 512 * h + 512],
-                    in_=obs[c][:, :, 512 * h : 512 * h + 512],
-                )
+                nc.scalar.activation(out=ob[:, :, ol * P : (ol + 1) * P], in_=pts[ol][:], func=ACT.Sin, scale=TWO_PI)
+                if i == NPAIR - 1:
+                    o0 = (2 * pr + ol) * P
+                    nc.sync.dma_start(out=oview[:, :, o0 : o0 + P], in_=ob[:, :, ol * P : (ol + 1) * P])
+            if i < NPAIR - 1:
+                nc.sync.dma_start(out=oview[:, :, 2 * pr * P : (2 * pr + 2) * P], in_=ob[:])
 
-        left_t(0)
-        weight_t(0)
-        w_unit(0, 0, 0)
-        w_unit(0, 1, 0)
-        x_step(0)
-        x_step(1)
-        weight_t(1)
-        w_unit(0, 0, 1)
-        w_unit(0, 1, 1)
-        x_step(2)
-        x_step(3)
-        weight_t(2)
-        w_unit(0, 0, 2)
-        w_unit(0, 1, 2)
-        x_step(4)
-        weight_t(3)
-        w_unit(0, 0, 3)
-        w_unit(0, 1, 3)
-        x_step(5)
-        left_t(1)
-        for i in range(NPAIR + 1):
-            if i < NPAIR:
-                s12(i)
-            if i >= 1:
-                s345(i - 1)
-            x_step(i + X_LEAD)
-            if i < 16 and i % 2 == 0:
-                w = i // 2
-                w_unit(1, w % 2, w // 2)
+        def n_w(i):
+            if i == -HEAD or i == -1:
+                return 1
+            if i < -1:
+                return 4
+            if i < 16:
+                return 1
+            return 0
+
+        def n_x(i):
+            if i == 2 - HEAD or i == 3 - HEAD:
+                return 2
+            if 4 - X_LEAD <= i < 4 * NCH - X_LEAD:
+                return 1
+            return 0
+
+        x_pos = {"s": 0}
+        for i in range(-HEAD, NPAIR + D_T):
+            head["on"] = i < -1
+            if 0 <= i < NPAIR:
+                s_mx(i)
+            for f in take(later_act):
+                f()
+            if 0 <= i < NPAIR:
+                s_u(i, False)
+            if 0 <= i - D_K < NPAIR:
+                s_k(i - D_K)
+            if 0 <= i - D_R < NPAIR:
+                s_r(i - D_R)
+            if 0 <= i < NPAIR:
+                s_u(i, True)
+            for f in take(later_dve):
+                f()
+            for f in take(pending):
+                f()
+            if 0 <= i - D_T < NPAIR:
+                s_out(i - D_T)
+            for j in range(max(n_w(i), n_x(i))):
+                if j < n_w(i):
+                    w_next()
+                if j < n_x(i):
+                    step_x(x_pos["s"])
+                    x_pos["s"] += 1

@@ -26,7 +26,7 @@ HEAD = 8
 HEAD_TAGS = ("a", "a", "y", "y", "t", "t")
 D_K, D_R, D_T = 1, 2, 3
 X_LEAD = 7
-U_DVE_FROM = 24
+U_DVE_FROM = 22
 
 
 def take(queue):
@@ -87,8 +87,8 @@ def tile_fmmlayer_t_kernel(tc, x, freq, phase_shift, weight, out):
 
         load_freq(0)
         load_w(0)
-        load_x(0)
         load_w(1)
+        load_x(0)
         load_w(2)
         load_w(3)
         load_freq(1)
@@ -148,10 +148,7 @@ def tile_fmmlayer_t_kernel(tc, x, freq, phase_shift, weight, out):
                     nc.tensor.transpose(pw[:, u, ol * P : (ol + 1) * P], wnf[:, ol, c0 : c0 + P], ident_f[:])
             dst = wThf[:, g, 256 * k : 256 * k + 256, :]
             src = pw[:].rearrange("p u o -> p o u")
-            if g == 0:
-                later_act.append(lambda: nc.scalar.copy(out=dst, in_=src))
-            else:
-                later_dve.append(lambda: nc.vector.tensor_copy(out=dst, in_=src))
+            later_act.append(lambda: nc.scalar.copy(out=dst, in_=src))
 
         th_now = {}
 
@@ -217,7 +214,10 @@ def tile_fmmlayer_t_kernel(tc, x, freq, phase_shift, weight, out):
 
         w_steps.append((False, lambda: step_halve(0)))
         w_steps.append((True, lambda: step_left(0)))
-        for k in range(4):
+        add_w(0, 0)
+        add_wt(0)
+        w_steps.append((False, lambda: step_halve(1)))
+        for k in range(1, 4):
             add_wt(k)
             if k < 3:
                 w_steps.append((False, lambda k=k: step_halve(k + 1)))
@@ -361,6 +361,10 @@ def tile_fmmlayer_t_kernel(tc, x, freq, phase_shift, weight, out):
         def n_w(i):
             if i == -HEAD or i == -1:
                 return 1
+            if i == 1 - HEAD:
+                return 6
+            if i == -2:
+                return 2
             if i < -1:
                 return 4
             if i < 16:

@@ -14,394 +14,412 @@ ACT = mybir.ActivationFunctionType
 ALU = mybir.AluOpType
 
 P = 128
-B, N, CI, CO, R = 2, 2048, 1024, 1024, 128
-FLOPS = 2 * B * N * CI * CO + 2 * B * CO * CI * R
-ROWS = N // P
-TQ = 4
-NCH = B * (ROWS // TQ)
-NPAIR = NCH * 4
+SAMPLES, ROWS, C_IN, C_OUT, RANK = 2, 2048, 1024, 1024, 128
+FLOPS = 2 * SAMPLES * ROWS * C_IN * C_OUT + 2 * SAMPLES * C_OUT * C_IN * RANK
+PASSES = C_IN // (4 * P)
+ROWS_PP = ROWS // P
+CHUNK_R = 4
+CHUNKS = SAMPLES * ROWS_PP // CHUNK_R
+PAIR = 2 * P
+PAIRS = C_OUT // PAIR
+UNITS = CHUNKS * PAIRS
+X_BANKS = 4 * CHUNKS
 TWO_PI = 2.0 * math.pi
 
 HEAD = 8
-HEAD_TAGS = ("a", "a", "y", "y", "t", "t")
-D_K, D_R, D_T = 1, 2, 3
+LAG_WHOLE, LAG_FRAC, LAG_OUT = 1, 2, 3
 X_LEAD = 7
-U_DVE_FROM = 22
+VECTOR_SCALES_FROM = 22
+HEAD_TAGS = ("w", "w", "y", "y", "t", "t")
 
 
-def take(queue):
-    items = list(queue)
-    queue[:] = []
-    return items
+def weight_banks(step):
+    if step == -HEAD:
+        return 1
+    if step == 1 - HEAD:
+        return len(HEAD_TAGS)
+    if step < -2:
+        return 4
+    if step == -2:
+        return 2
+    if step < 4 * PAIRS:
+        return 1
+    return 0
+
+
+def x_banks(step):
+    if step in (2 - HEAD, 3 - HEAD):
+        return 2
+    if 4 - X_LEAD <= step < X_BANKS - X_LEAD:
+        return 1
+    return 0
+
+
+def due(table, step, work):
+    if step not in table:
+        table[step] = []
+    table[step].append(work)
 
 
 def tile_fmmlayer_t_kernel(tc, x, freq, phase_shift, weight, out):
     nc = tc.nc
     with ExitStack() as ctx:
         keep = ctx.enter_context(tc.tile_pool(name="keep", bufs=1))
-        xs_pool = ctx.enter_context(tc.tile_pool(name="xs", bufs=4))
-        st2 = ctx.enter_context(tc.tile_pool(name="st2", bufs=2))
-        st3 = ctx.enter_context(tc.tile_pool(name="st3", bufs=3))
-        st4 = ctx.enter_context(tc.tile_pool(name="st4", bufs=4))
+        two = ctx.enter_context(tc.tile_pool(name="two", bufs=2))
+        three = ctx.enter_context(tc.tile_pool(name="three", bufs=3))
+        four = ctx.enter_context(tc.tile_pool(name="four", bufs=4))
         psum = ctx.enter_context(tc.psum_pool(name="psum", bufs=2))
         ctx.enter_context(tc.manual_schedule())
 
-        ident_b = keep.tile([P, P], BF16, name="ident_b")
-        make_identity(nc, ident_b[:])
-        ident_f = keep.tile([P, P], F32, name="ident_f")
-        make_identity(nc, ident_f[:])
-        warm_in = keep.tile([P, 1], F32, name="warm_in")
-        nc.vector.memset(warm_in[:], 0.0)
-        warm_out = keep.tile([P, 1], F32, name="warm_out")
-        nc.scalar.activation(out=warm_out[:], in_=warm_in[:], func=ACT.Silu)
+        ident_bf16 = keep.tile([P, P], BF16, name="ident_bf16")
+        make_identity(nc, ident_bf16[:])
+        ident_f32 = keep.tile([P, P], F32, name="ident_f32")
+        make_identity(nc, ident_f32[:])
+        zero_col = keep.tile([P, 1], F32, name="zero_col")
+        nc.vector.memset(zero_col[:], 0.0)
+        silu_col = keep.tile([P, 1], F32, name="silu_col")
+        nc.scalar.activation(out=silu_col[:], in_=zero_col[:], func=ACT.Silu)
 
-        psz = keep.tile([P, P], BF16, name="psz")
-        nc.vector.memset(psz[:], 0.0)
-        nc.sync.dma_start(out=psz[0:32, :], in_=phase_shift.rearrange("b (r c) -> (b r) c", c=P))
-        lf = []
-        rt = []
-        wn = []
-        for b in range(B):
-            lf.append(keep.tile([P, 8, R], BF16, name="lf%d" % b))
-            rt.append(keep.tile([P, CI], BF16, name="rt%d" % b))
-        for k in range(4):
-            wn.append(keep.tile([P, 2, CI], BF16, name="wn%d" % k))
-        wview = weight.rearrange("(t p) i -> p t i", p=P)
+        shift_rows = keep.tile([P, P], BF16, name="shift_rows")
+        nc.vector.memset(shift_rows[:], 0.0)
+        nc.sync.dma_start(out=shift_rows[0:32, :], in_=phase_shift.rearrange("b (n w) -> (b n) w", w=P))
+        left = []
+        right = []
+        for b in range(SAMPLES):
+            left.append(keep.tile([P, C_OUT // P, RANK], BF16, name="left%d" % b))
+            right.append(keep.tile([P, C_IN], BF16, name="right%d" % b))
+        w_rows = []
+        for k in range(PAIRS):
+            w_rows.append(keep.tile([P, 2, C_IN], BF16, name="w_rows%d" % k))
 
-        def load_freq(b):
-            nc.sync.dma_start(out=lf[b][:], in_=freq[b, 0 : CO * R].rearrange("(t p r) -> p t r", t=8, p=P))
-            nc.sync.dma_start(out=rt[b][:], in_=freq[b, CO * R : CO * R + R * CI].rearrange("(r i) -> r i", r=R))
+        def load_factors(b):
+            nc.sync.dma_start(out=left[b][:], in_=freq[b, 0 : C_OUT * RANK].rearrange("(t p r) -> p t r", p=P, r=RANK))
+            nc.sync.dma_start(
+                out=right[b][:], in_=freq[b, C_OUT * RANK : (C_OUT + C_IN) * RANK].rearrange("(r i) -> r i", r=RANK)
+            )
 
-        def load_w(k):
-            nc.sync.dma_start(out=wn[k][:], in_=wview[:, 2 * k : 2 * k + 2, :])
+        def load_weight(k):
+            nc.sync.dma_start(out=w_rows[k][:], in_=weight.rearrange("(t p) i -> p t i", p=P)[:, 2 * k : 2 * k + 2, :])
 
-        xs = {}
+        x_rows = {}
 
         def load_x(c):
-            b, q = divmod(c, 4)
-            xs_t = xs_pool.tile([P, TQ, CI], BF16, name="xs_t", tag="xs")
+            b, q = divmod(c, CHUNKS // SAMPLES)
+            x_chunk = four.tile([P, CHUNK_R, C_IN], BF16, name="x_chunk")
             nc.sync.dma_start(
-                out=xs_t[:], in_=x[b].rearrange("(j s) i -> j s i", s=ROWS)[:, TQ * q : TQ * q + TQ, :]
+                out=x_chunk[:],
+                in_=x[b].rearrange("(j s) i -> j s i", s=ROWS_PP)[:, CHUNK_R * q : CHUNK_R * (q + 1), :],
             )
-            xs[c] = xs_t
+            x_rows[c] = x_chunk
 
-        load_freq(0)
-        load_w(0)
-        load_w(1)
+        load_factors(0)
+        load_weight(0)
+        load_weight(1)
         load_x(0)
-        load_w(2)
-        load_w(3)
-        load_freq(1)
-        load_x(1)
-        load_x(2)
-        load_x(3)
+        load_weight(2)
+        load_weight(3)
+        load_factors(1)
+        for c in range(1, 4):
+            load_x(c)
 
-        later_act = []
-        later_dve = []
-        pending = []
-        head = {"on": False, "n": 0}
+        scalar_due = {}
+        copy_due = {}
+        product_due = {}
+        w_quantise_due = {}
+        x_quantise_due = {}
+        head_banks = {"on": False, "used": 0}
 
-        def w_bank(shape, dtype):
-            tag = "a"
-            if head["on"]:
-                tag = HEAD_TAGS[head["n"] % len(HEAD_TAGS)]
-                head["n"] += 1
-            wb = psum.tile(shape, dtype, name="wb", tag=tag)
-            return wb
+        def weight_bank(shape, dtype):
+            tag = "w"
+            if head_banks["on"]:
+                tag = HEAD_TAGS[head_banks["used"] % len(HEAD_TAGS)]
+                head_banks["used"] += 1
+            bank = psum.tile(shape, dtype, name="bank", tag=tag)
+            return bank
 
-        pps = w_bank([P, P], BF16)
-        nc.tensor.transpose(pps[:], psz[:], ident_b[:])
-        psv = pps[:, 0:32].rearrange("p (b h o) -> p b h o", b=B, h=2)
-        fs2 = keep.tile([P, B, 8], F32, name="fs2")
-        ph2 = keep.tile([P, B, 8], F32, name="ph2")
-        nc.vector.tensor_scalar(out=fs2[:], in0=psv[:, :, 0, :], scalar1=1.0 / TWO_PI, scalar2=None, op0=ALU.mult)
+        shift_cols = weight_bank([P, P], BF16)
+        nc.tensor.transpose(shift_cols[:], shift_rows[:], ident_bf16[:])
+        halves = shift_cols[:, 0:32].rearrange("p (b f t) -> p b f t", b=SAMPLES, f=2)
+        scale_turns = keep.tile([P, SAMPLES, C_OUT // P], F32, name="scale_turns")
+        phase_turns = keep.tile([P, SAMPLES, C_OUT // P], F32, name="phase_turns")
         nc.vector.tensor_scalar(
-            out=ph2[:], in0=psv[:, :, 1, :], scalar1=-30.0, scalar2=1.0 / (15.0 * TWO_PI), op0=ALU.add, op1=ALU.mult
+            out=scale_turns[:], in0=halves[:, :, 0, :], scalar1=1.0 / TWO_PI, scalar2=None, op0=ALU.mult
+        )
+        nc.vector.tensor_scalar(
+            out=phase_turns[:],
+            in0=halves[:, :, 1, :],
+            scalar1=-30.0,
+            scalar2=1.0 / (15.0 * TWO_PI),
+            op0=ALU.add,
+            op1=ALU.mult,
         )
 
-        lT = []
-        wc = []
-        wsc = []
-        for b in range(B):
-            lT.append(keep.tile([P, CO], BF16, name="lT%d" % b))
-            wc.append(keep.tile([P, 2, CO], U32, name="wc%d" % b, align_bytes=64))
-            wsc.append(keep.tile([P, 2, CO], U8, name="wsc%d" % b, align_bytes=64))
-        wTh = keep.tile([P, 2, CO, 4], BF16, name="wTh")
-        wThf = wTh[:].bitcast(F32)
+        left_t = []
+        w_codes = []
+        w_scales = []
+        for b in range(SAMPLES):
+            left_t.append(keep.tile([P, C_OUT], BF16, name="left_t%d" % b))
+            w_codes.append(keep.tile([P, PASSES, C_OUT], U32, name="w_codes%d" % b, align_bytes=64))
+            w_scales.append(keep.tile([P, PASSES, C_OUT], U8, name="w_scales%d" % b, align_bytes=64))
+        half_w = keep.tile([P, PASSES, C_OUT, 4], BF16, name="half_w")
+        half_w_words = half_w[:].bitcast(F32)
 
-        def step_left(b):
-            plf = w_bank([P, 8, P], BF16)
-            for t in range(8):
-                nc.tensor.transpose(plf[:, t, :], lf[b][:, t, :], ident_b[:])
-            later_act.append(lambda: nc.scalar.copy(out=lT[b][:], in_=plf[:].rearrange("p t o -> p (t o)")))
+        def transpose_left(b, step):
+            bank = weight_bank([P, C_OUT // P, P], BF16)
+            for t in range(C_OUT // P):
+                nc.tensor.transpose(bank[:, t, :], left[b][:, t, :], ident_bf16[:])
+            due(scalar_due, step + 1, lambda: nc.scalar.copy(out=left_t[b][:], in_=bank[:].rearrange("p t o -> p (t o)")))
 
-        def step_halve(k):
-            flat = wn[k][:].rearrange("p t i -> p (t i)")
+        def halve_weight(k):
+            flat = w_rows[k][:].rearrange("p t i -> p (t i)")
             nc.vector.tensor_scalar(out=flat, in0=flat, scalar1=0.5, scalar2=None, op0=ALU.mult)
 
-        def step_wt(k, g):
-            wnf = wn[k][:].bitcast(F32)
-            pw = w_bank([P, 2, 256], F32)
-            for u in range(2):
-                for ol in range(2):
-                    c0 = 256 * g + 128 * u
-                    nc.tensor.transpose(pw[:, u, ol * P : (ol + 1) * P], wnf[:, ol, c0 : c0 + P], ident_f[:])
-            dst = wThf[:, g, 256 * k : 256 * k + 256, :]
-            src = pw[:].rearrange("p u o -> p o u")
-            later_act.append(lambda: nc.scalar.copy(out=dst, in_=src))
+        def transpose_weight(k, g, step):
+            words = w_rows[k][:].bitcast(F32)
+            bank = weight_bank([P, 2, PAIR], F32)
+            for h in range(2):
+                for t in range(2):
+                    first = 256 * g + P * h
+                    nc.tensor.transpose(bank[:, h, t * P : (t + 1) * P], words[:, t, first : first + P], ident_f32[:])
+            due(
+                scalar_due,
+                step + 1,
+                lambda: nc.scalar.copy(
+                    out=half_w_words[:, g, PAIR * k : PAIR * (k + 1), :], in_=bank[:].rearrange("p h o -> p o h")
+                ),
+            )
 
-        th_now = {}
+        tanh_tiles = {}
+        w_grouped = {}
 
-        def step_w(b, g, oq, ol):
-            if ol == 0:
-                th_new = st3.tile([P, 256, 4], F32, name="th_new", tag="th")
-                th_now["t"] = th_new
-            th = th_now["t"]
-            ot = 2 * oq + ol
-            rtv = rt[b][:].rearrange("r (g u p e) -> r g u e p", g=2, u=2, p=P, e=2)
-            pm = w_bank([P, 4, P], F32)
-            for u in range(2):
+        def modulate(b, g, k, t, step):
+            if t == 0:
+                tanh_tile = three.tile([P, PAIR, 4], F32, name="tanh_tile")
+                tanh_tiles[(b, g, k)] = tanh_tile
+            tanh_pair = tanh_tiles[(b, g, k)]
+            first = (2 * k + t) * P
+            columns = right[b][:].rearrange("r (g h p e) -> r g h e p", g=PASSES, h=2, e=2)
+            bank = weight_bank([P, 4, P], F32)
+            for h in range(2):
                 for e in range(2):
                     nc.tensor.matmul(
-                        out=pm[:, 2 * u + e, :],
-                        lhsT=rtv[:, g, u, e, :],
-                        rhs=lT[b][:, ot * P : (ot + 1) * P],
+                        out=bank[:, 2 * h + e, :],
+                        lhsT=columns[:, g, h, e, :],
+                        rhs=left_t[b][:, first : first + P],
                         start=True,
                         stop=True,
                     )
-
-            def quant(gw):
-                nc.vector.quantize_mx(
-                    out=wc[b][:, g, 256 * oq : 256 * oq + 256].bitcast(FP8X4),
-                    scales=wsc[b][:, g, 256 * oq : 256 * oq + 256],
-                    in_=gw[:].rearrange("p o t -> p (o t)"),
-                )
-
-            def modulate():
-                gw = st2.tile([P, 256, 4], BF16, name="gw", tag="gw", align_bytes=64)
-                nc.vector.scalar_tensor_tensor(
-                    out=gw[:].rearrange("p o t -> p (o t)"),
-                    in0=th[:].rearrange("p o t -> p (o t)"),
-                    scalar=2.0,
-                    in1=wTh[:, g, 256 * oq : 256 * oq + 256, :].rearrange("p o t -> p (o t)"),
-                    op0=ALU.add,
-                    op1=ALU.mult,
-                )
-                pending.append(lambda: quant(gw))
-
-            def tanh():
-                nc.scalar.activation(
-                    out=th[:, ol * P : (ol + 1) * P, :],
-                    in_=pm[:].rearrange("p t o -> p o t"),
+            due(
+                scalar_due,
+                step + 1,
+                lambda: nc.scalar.activation(
+                    out=tanh_pair[:, t * P : (t + 1) * P, :],
+                    in_=bank[:].rearrange("p v o -> p o v"),
                     func=ACT.Tanh,
-                    scale=0.5 / math.sqrt(R),
-                )
-                if ol == 1:
-                    pending.append(modulate)
+                    scale=0.5 / math.sqrt(RANK),
+                ),
+            )
+            if t == 1:
+                due(product_due, step + 1, lambda: product(b, g, k))
+                due(w_quantise_due, step + 2, lambda: quantise_weight(b, g, k))
 
-            later_act.append(tanh)
+        def product(b, g, k):
+            grouped = two.tile([P, PAIR, 4], BF16, name="grouped", align_bytes=64)
+            nc.vector.scalar_tensor_tensor(
+                out=grouped[:].rearrange("p o v -> p (o v)"),
+                in0=tanh_tiles[(b, g, k)][:].rearrange("p o v -> p (o v)"),
+                scalar=2.0,
+                in1=half_w[:, g, PAIR * k : PAIR * (k + 1), :].rearrange("p o v -> p (o v)"),
+                op0=ALU.add,
+                op1=ALU.mult,
+            )
+            w_grouped[(b, g, k)] = grouped
 
-        w_steps = []
-
-        def add_w(b, oq):
-            for g in range(2):
-                for ol in range(2):
-                    w_steps.append((True, lambda g=g, ol=ol: step_w(b, g, oq, ol)))
-
-        def add_wt(k):
-            for g in range(2):
-                w_steps.append((True, lambda g=g: step_wt(k, g)))
-
-        w_steps.append((False, lambda: step_halve(0)))
-        w_steps.append((True, lambda: step_left(0)))
-        add_w(0, 0)
-        add_wt(0)
-        w_steps.append((False, lambda: step_halve(1)))
-        for k in range(1, 4):
-            add_wt(k)
-            if k < 3:
-                w_steps.append((False, lambda k=k: step_halve(k + 1)))
-            add_w(0, k)
-        w_steps.append((True, lambda: step_left(1)))
-        for k in range(4):
-            add_w(1, k)
-        w_pos = {"i": 0}
-
-        def w_free():
-            while w_pos["i"] < len(w_steps) and not w_steps[w_pos["i"]][0]:
-                w_steps[w_pos["i"]][1]()
-                w_pos["i"] += 1
-
-        def w_next():
-            w_free()
-            w_steps[w_pos["i"]][1]()
-            w_pos["i"] += 1
-            w_free()
-
-        xc = {}
-        xsc = {}
-        gx = {}
-
-        def x_quant(c, g):
+        def quantise_weight(b, g, k):
             nc.vector.quantize_mx(
-                out=xc[c][:, g, :].bitcast(FP8X4),
-                scales=xsc[c][:, g, :],
-                in_=gx[(c, g)][:].rearrange("p n t -> p (n t)"),
+                out=w_codes[b][:, g, PAIR * k : PAIR * (k + 1)].bitcast(FP8X4),
+                scales=w_scales[b][:, g, PAIR * k : PAIR * (k + 1)],
+                in_=w_grouped[(b, g, k)][:].rearrange("p o v -> p (o v)"),
             )
 
-        def step_x(s):
-            c, sub = divmod(s, 4)
-            g, tp = divmod(sub, 2)
-            if sub == 0:
-                xc_t = st3.tile([P, 2, 512], U32, name="xc_t", tag="xc", align_bytes=64)
-                xsc_t = st3.tile([P, 2, 512], U8, name="xsc_t", tag="xsc", align_bytes=64)
-                xc[c] = xc_t
-                xsc[c] = xsc_t
-            if tp == 0:
-                gx_t = st4.tile([P, 512, 4], BF16, name="gx_t", tag="gx", align_bytes=64)
-                gx[(c, g)] = gx_t
-            xf = xs[c][:].bitcast(F32)
-            px = psum.tile([P, 2, 256], F32, name="px", tag="x")
-            for u in range(2):
-                for tl in range(2):
-                    c0 = 256 * g + 128 * u
-                    nc.tensor.transpose(px[:, u, tl * P : (tl + 1) * P], xf[:, 2 * tp + tl, c0 : c0 + P], ident_f[:])
-            dst = gx[(c, g)][:].bitcast(F32)[:, 256 * tp : 256 * tp + 256, :]
-            src = px[:].rearrange("p u n -> p n u")
-            if s % 2 == 0:
-                later_act.append(lambda: nc.scalar.copy(out=dst, in_=src))
-            else:
-                later_dve.append(lambda: nc.vector.tensor_copy(out=dst, in_=src))
-            if sub == 3 and c + 4 < NCH:
-                load_x(c + 4)
-            if tp == 1:
-                later_dve.append(lambda: pending.append(lambda: pending.append(lambda: x_quant(c, g))))
+        stream = []
 
-        ys = {}
-        us = {}
-        ks = {}
-        rs = {}
+        def add_modulation(b, k):
+            for g in range(PASSES):
+                for t in range(2):
+                    stream.append((True, lambda step, g=g, t=t: modulate(b, g, k, t, step)))
 
-        def where(i):
-            c, pr = divmod(i, 4)
-            b, q = divmod(c, 4)
-            return b, q, c, pr
+        def add_weight(k):
+            for g in range(PASSES):
+                stream.append((True, lambda step, g=g: transpose_weight(k, g, step)))
 
-        def s_mx(i):
-            b, q, c, pr = where(i)
-            for ol in range(2):
-                ot = 2 * pr + ol
-                py = psum.tile([P, 512], F32, name="py", tag="y")
-                for g in range(2):
-                    nc.tensor.matmul_mx(
-                        out=py[:],
-                        lhsT=wc[b][:, g, ot * P : (ot + 1) * P].bitcast(FP8X4),
-                        lhsT_scale=wsc[b][:, g, ot * P : (ot + 1) * P],
-                        rhs=xc[c][:, g, :].bitcast(FP8X4),
-                        rhs_scale=xsc[c][:, g, :],
-                        start=(g == 0),
-                        stop=(g == 1),
+        stream.append((False, lambda step: halve_weight(0)))
+        stream.append((True, lambda step: transpose_left(0, step)))
+        add_modulation(0, 0)
+        add_weight(0)
+        stream.append((False, lambda step: halve_weight(1)))
+        for k in range(1, PAIRS):
+            add_weight(k)
+            if k + 1 < PAIRS:
+                stream.append((False, lambda step, k=k: halve_weight(k + 1)))
+            add_modulation(0, k)
+        stream.append((True, lambda step: transpose_left(1, step)))
+        for k in range(PAIRS):
+            add_modulation(1, k)
+        position = {"stream": 0, "x": 0}
+
+        def halvings(step):
+            while position["stream"] < len(stream) and not stream[position["stream"]][0]:
+                stream[position["stream"]][1](step)
+                position["stream"] += 1
+
+        def next_weight_bank(step):
+            halvings(step)
+            stream[position["stream"]][1](step)
+            position["stream"] += 1
+            halvings(step)
+
+        x_codes = {}
+        x_scales = {}
+        x_grouped = {}
+
+        def quantise_x(c, g):
+            nc.vector.quantize_mx(
+                out=x_codes[c][:, g, :].bitcast(FP8X4),
+                scales=x_scales[c][:, g, :],
+                in_=x_grouped[(c, g)][:].rearrange("p n v -> p (n v)"),
+            )
+
+        def next_x_bank(step):
+            number = position["x"]
+            position["x"] += 1
+            c, g, rows_half = number // 4, number // 2 % 2, number % 2
+            if number % 4 == 0:
+                codes = three.tile([P, PASSES, 4 * P], U32, name="codes", align_bytes=64)
+                scales = three.tile([P, PASSES, 4 * P], U8, name="scales", align_bytes=64)
+                x_codes[c] = codes
+                x_scales[c] = scales
+            if rows_half == 0:
+                regrouped = four.tile([P, 4 * P, 4], BF16, name="regrouped", align_bytes=64)
+                x_grouped[(c, g)] = regrouped
+            words = x_rows[c][:].bitcast(F32)
+            bank = psum.tile([P, 2, PAIR], F32, name="x_bank", tag="x")
+            for h in range(2):
+                for r in range(2):
+                    first = 256 * g + P * h
+                    nc.tensor.transpose(
+                        bank[:, h, r * P : (r + 1) * P], words[:, 2 * rows_half + r, first : first + P], ident_f32[:]
                     )
-                ys[(i, ol)] = py
-            u_t = st4.tile([P, 2, 512], F32, name="u_t", tag="u")
-            us[i] = u_t
+            target = x_grouped[(c, g)][:].bitcast(F32)[:, PAIR * rows_half : PAIR * (rows_half + 1), :]
+            source = bank[:].rearrange("p h n -> p n h")
+            if rows_half == 0:
+                due(scalar_due, step + 1, lambda: nc.scalar.copy(out=target, in_=source))
+            else:
+                due(copy_due, step + 1, lambda: nc.vector.tensor_copy(out=target, in_=source))
+                due(x_quantise_due, step + 2, lambda: quantise_x(c, g))
+            if number % 4 == 3 and c + 4 < CHUNKS:
+                load_x(c + 4)
 
-        def s_u(i, on_dve):
-            b, q, c, pr = where(i)
-            for ol in range(2):
-                ot = 2 * pr + ol
-                if (i >= U_DVE_FROM and i % 2 == 0 and ol == 1) != on_dve:
+        y_banks = {}
+        turns = {}
+        whole = {}
+        frac = {}
+
+        def multiply(unit):
+            c, k = divmod(unit, PAIRS)
+            b = c // (CHUNKS // SAMPLES)
+            for t in range(2):
+                first = (2 * k + t) * P
+                y_bank = psum.tile([P, 4 * P], F32, name="y_bank", tag="y")
+                for g in range(PASSES):
+                    nc.tensor.matmul_mx(
+                        out=y_bank[:],
+                        lhsT=w_codes[b][:, g, first : first + P].bitcast(FP8X4),
+                        lhsT_scale=w_scales[b][:, g, first : first + P],
+                        rhs=x_codes[c][:, g, :].bitcast(FP8X4),
+                        rhs_scale=x_scales[c][:, g, :],
+                        start=(g == 0),
+                        stop=(g == PASSES - 1),
+                    )
+                y_banks[(unit, t)] = y_bank
+            turns_tile = four.tile([P, 2, 4 * P], F32, name="turns_tile")
+            turns[unit] = turns_tile
+
+        def scale_and_shift(unit, on_vector):
+            c, k = divmod(unit, PAIRS)
+            b = c // (CHUNKS // SAMPLES)
+            for t in range(2):
+                tile_index = 2 * k + t
+                if (unit >= VECTOR_SCALES_FROM and unit % 2 == 0 and t == 1) != on_vector:
                     continue
-                if on_dve:
+                if on_vector:
                     nc.vector.tensor_scalar(
-                        out=us[i][:, ol, :],
-                        in0=ys[(i, ol)][:],
-                        scalar1=fs2[:, b, ot : ot + 1],
-                        scalar2=ph2[:, b, ot : ot + 1],
+                        out=turns[unit][:, t, :],
+                        in0=y_banks[(unit, t)][:],
+                        scalar1=scale_turns[:, b, tile_index : tile_index + 1],
+                        scalar2=phase_turns[:, b, tile_index : tile_index + 1],
                         op0=ALU.mult,
                         op1=ALU.add,
                     )
                 else:
                     nc.scalar.activation(
-                        out=us[i][:, ol, :],
-                        in_=ys[(i, ol)][:],
+                        out=turns[unit][:, t, :],
+                        in_=y_banks[(unit, t)][:],
                         func=ACT.Identity,
-                        scale=fs2[:, b, ot : ot + 1],
-                        bias=ph2[:, b, ot : ot + 1],
+                        scale=scale_turns[:, b, tile_index : tile_index + 1],
+                        bias=phase_turns[:, b, tile_index : tile_index + 1],
                     )
 
-        def s_k(i):
-            k_t = st3.tile([P, 2, 512], I32, name="k_t", tag="k")
-            nc.vector.tensor_copy(out=k_t[:], in_=us[i][:])
-            ks[i] = k_t
+        def round_turns(unit):
+            whole_tile = three.tile([P, 2, 4 * P], I32, name="whole_tile")
+            nc.vector.tensor_copy(out=whole_tile[:], in_=turns[unit][:])
+            whole[unit] = whole_tile
 
-        def s_r(i):
-            r_t = st3.tile([P, 2, 512], F32, name="r_t", tag="r")
-            nc.vector.tensor_tensor(out=r_t[:], in0=us[i][:], in1=ks[i][:], op=ALU.subtract)
-            rs[i] = r_t
+        def subtract_whole(unit):
+            frac_tile = three.tile([P, 2, 4 * P], F32, name="frac_tile")
+            nc.vector.tensor_tensor(out=frac_tile[:], in0=turns[unit][:], in1=whole[unit][:], op=ALU.subtract)
+            frac[unit] = frac_tile
 
-        def s_out(i):
-            b, q, c, pr = where(i)
-            pts = []
-            for ol in range(2):
-                pt = psum.tile([P, TQ, P], F32, name="pt", tag="t")
-                for t in range(TQ):
-                    nc.tensor.transpose(pt[:, t, :], rs[i][:, ol, t * P : (t + 1) * P], ident_f[:])
-                pts.append(pt)
-            ob = st3.tile([P, TQ, 2 * P], F32, name="ob", tag="ob")
-            oview = out[b].rearrange("(j s) o -> j s o", s=ROWS)[:, TQ * q : TQ * q + TQ, :]
-            for ol in range(2):
-                nc.scalar.activation(out=ob[:, :, ol * P : (ol + 1) * P], in_=pts[ol][:], func=ACT.Sin, scale=TWO_PI)
-                if i == NPAIR - 1:
-                    o0 = (2 * pr + ol) * P
-                    nc.sync.dma_start(out=oview[:, :, o0 : o0 + P], in_=ob[:, :, ol * P : (ol + 1) * P])
-            if i < NPAIR - 1:
-                nc.sync.dma_start(out=oview[:, :, 2 * pr * P : (2 * pr + 2) * P], in_=ob[:])
+        def sine_and_store(unit):
+            c, k = divmod(unit, PAIRS)
+            b, q = divmod(c, CHUNKS // SAMPLES)
+            t_banks = []
+            for t in range(2):
+                t_bank = psum.tile([P, CHUNK_R, P], F32, name="t_bank", tag="t")
+                for r in range(CHUNK_R):
+                    nc.tensor.transpose(t_bank[:, r, :], frac[unit][:, t, r * P : (r + 1) * P], ident_f32[:])
+                t_banks.append(t_bank)
+            result = three.tile([P, CHUNK_R, PAIR], F32, name="result")
+            rows = out[b].rearrange("(j s) o -> j s o", s=ROWS_PP)[:, CHUNK_R * q : CHUNK_R * (q + 1), :]
+            for t in range(2):
+                nc.scalar.activation(out=result[:, :, t * P : (t + 1) * P], in_=t_banks[t][:], func=ACT.Sin, scale=TWO_PI)
+                if unit == UNITS - 1:
+                    first = PAIR * k + t * P
+                    nc.sync.dma_start(out=rows[:, :, first : first + P], in_=result[:, :, t * P : (t + 1) * P])
+            if unit < UNITS - 1:
+                nc.sync.dma_start(out=rows[:, :, PAIR * k : PAIR * (k + 1)], in_=result[:])
 
-        def n_w(i):
-            if i == -HEAD or i == -1:
-                return 1
-            if i == 1 - HEAD:
-                return 6
-            if i == -2:
-                return 2
-            if i < -1:
-                return 4
-            if i < 16:
-                return 1
-            return 0
-
-        def n_x(i):
-            if i == 2 - HEAD or i == 3 - HEAD:
-                return 2
-            if 4 - X_LEAD <= i < 4 * NCH - X_LEAD:
-                return 1
-            return 0
-
-        x_pos = {"s": 0}
-        for i in range(-HEAD, NPAIR + D_T):
-            head["on"] = i < -1
-            if 0 <= i < NPAIR:
-                s_mx(i)
-            for f in take(later_act):
-                f()
-            if 0 <= i < NPAIR:
-                s_u(i, False)
-            if 0 <= i - D_K < NPAIR:
-                s_k(i - D_K)
-            if 0 <= i - D_R < NPAIR:
-                s_r(i - D_R)
-            if 0 <= i < NPAIR:
-                s_u(i, True)
-            for f in take(later_dve):
-                f()
-            for f in take(pending):
-                f()
-            if 0 <= i - D_T < NPAIR:
-                s_out(i - D_T)
-            for j in range(max(n_w(i), n_x(i))):
-                if j < n_w(i):
-                    w_next()
-                if j < n_x(i):
-                    step_x(x_pos["s"])
-                    x_pos["s"] += 1
+        for step in range(-HEAD, UNITS + LAG_OUT):
+            head_banks["on"] = step < -1
+            if 0 <= step < UNITS:
+                multiply(step)
+            for work in scalar_due.get(step, []):
+                work()
+            if 0 <= step < UNITS:
+                scale_and_shift(step, False)
+            if 0 <= step - LAG_WHOLE < UNITS:
+                round_turns(step - LAG_WHOLE)
+            if 0 <= step - LAG_FRAC < UNITS:
+                subtract_whole(step - LAG_FRAC)
+            if 0 <= step < UNITS:
+                scale_and_shift(step, True)
+            for table in (copy_due, w_quantise_due, x_quantise_due, product_due):
+                for work in table.get(step, []):
+                    work()
+            if 0 <= step - LAG_OUT < UNITS:
+                sine_and_store(step - LAG_OUT)
+            for turn in range(max(weight_banks(step), x_banks(step))):
+                if turn < weight_banks(step):
+                    next_weight_bank(step)
+                if turn < x_banks(step):
+                    next_x_bank(step)

import math
from contextlib import ExitStack

import concourse.mybir as mybir
from concourse.masks import make_identity

F32 = mybir.dt.float32
BF16 = mybir.dt.bfloat16
I32 = mybir.dt.int32
U32 = mybir.dt.uint32
U8 = mybir.dt.uint8
FP8X4 = mybir.dt.float8_e4m3fn_x4
ACT = mybir.ActivationFunctionType
ALU = mybir.AluOpType

P = 128
SAMPLES, ROWS, C_IN, C_OUT, RANK = 2, 2048, 1024, 1024, 128
FLOPS = 2 * SAMPLES * ROWS * C_IN * C_OUT + 2 * SAMPLES * C_OUT * C_IN * RANK
PASSES = C_IN // (4 * P)
ROWS_PP = ROWS // P
CHUNK_R = 4
CHUNKS = SAMPLES * ROWS_PP // CHUNK_R
PAIR = 2 * P
PAIRS = C_OUT // PAIR
UNITS = CHUNKS * PAIRS
X_BANKS = 4 * CHUNKS
TWO_PI = 2.0 * math.pi

HEAD = 8
LAG_WHOLE, LAG_FRAC, LAG_OUT = 1, 2, 3
X_LEAD = 7
VECTOR_SCALES_FROM = 22
HEAD_TAGS = ("w", "w", "y", "y", "t", "t")


def weight_banks(step):
    if step == -HEAD:
        return 1
    if step == 1 - HEAD:
        return len(HEAD_TAGS)
    if step < -2:
        return 4
    if step == -2:
        return 2
    if step < 4 * PAIRS:
        return 1
    return 0


def x_banks(step):
    if step in (2 - HEAD, 3 - HEAD):
        return 2
    if 4 - X_LEAD <= step < X_BANKS - X_LEAD:
        return 1
    return 0


def due(table, step, work):
    if step not in table:
        table[step] = []
    table[step].append(work)


def tile_fmmlayer_t_kernel(tc, x, freq, phase_shift, weight, out):
    nc = tc.nc
    with ExitStack() as ctx:
        keep = ctx.enter_context(tc.tile_pool(name="keep", bufs=1))
        two = ctx.enter_context(tc.tile_pool(name="two", bufs=2))
        three = ctx.enter_context(tc.tile_pool(name="three", bufs=3))
        four = ctx.enter_context(tc.tile_pool(name="four", bufs=4))
        psum = ctx.enter_context(tc.psum_pool(name="psum", bufs=2))
        ctx.enter_context(tc.manual_schedule())

        ident_bf16 = keep.tile([P, P], BF16, name="ident_bf16")
        make_identity(nc, ident_bf16[:])
        ident_f32 = keep.tile([P, P], F32, name="ident_f32")
        make_identity(nc, ident_f32[:])
        zero_col = keep.tile([P, 1], F32, name="zero_col")
        nc.vector.memset(zero_col[:], 0.0)
        silu_col = keep.tile([P, 1], F32, name="silu_col")
        nc.scalar.activation(out=silu_col[:], in_=zero_col[:], func=ACT.Silu)

        shift_rows = keep.tile([P, P], BF16, name="shift_rows")
        nc.vector.memset(shift_rows[:], 0.0)
        nc.sync.dma_start(out=shift_rows[0:32, :], in_=phase_shift.rearrange("b (n w) -> (b n) w", w=P))
        left = []
        right = []
        for b in range(SAMPLES):
            left.append(keep.tile([P, C_OUT // P, RANK], BF16, name="left%d" % b))
            right.append(keep.tile([P, C_IN], BF16, name="right%d" % b))
        w_rows = []
        for k in range(PAIRS):
            w_rows.append(keep.tile([P, 2, C_IN], BF16, name="w_rows%d" % k))

        def load_factors(b):
            nc.sync.dma_start(out=left[b][:], in_=freq[b, 0 : C_OUT * RANK].rearrange("(t p r) -> p t r", p=P, r=RANK))
            nc.sync.dma_start(
                out=right[b][:], in_=freq[b, C_OUT * RANK : (C_OUT + C_IN) * RANK].rearrange("(r i) -> r i", r=RANK)
            )

        def load_weight(k):
            nc.sync.dma_start(out=w_rows[k][:], in_=weight.rearrange("(t p) i -> p t i", p=P)[:, 2 * k : 2 * k + 2, :])

        x_rows = {}

        def load_x(c):
            b, q = divmod(c, CHUNKS // SAMPLES)
            x_chunk = four.tile([P, CHUNK_R, C_IN], BF16, name="x_chunk")
            nc.sync.dma_start(
                out=x_chunk[:],
                in_=x[b].rearrange("(j s) i -> j s i", s=ROWS_PP)[:, CHUNK_R * q : CHUNK_R * (q + 1), :],
            )
            x_rows[c] = x_chunk

        load_factors(0)
        load_weight(0)
        load_weight(1)
        load_x(0)
        load_weight(2)
        load_weight(3)
        load_factors(1)
        for c in range(1, 4):
            load_x(c)

        scalar_due = {}
        copy_due = {}
        product_due = {}
        w_quantise_due = {}
        x_quantise_due = {}
        head_banks = {"on": False, "used": 0}

        def weight_bank(shape, dtype):
            tag = "w"
            if head_banks["on"]:
                tag = HEAD_TAGS[head_banks["used"] % len(HEAD_TAGS)]
                head_banks["used"] += 1
            bank = psum.tile(shape, dtype, name="bank", tag=tag)
            return bank

        shift_cols = weight_bank([P, P], BF16)
        nc.tensor.transpose(shift_cols[:], shift_rows[:], ident_bf16[:])
        halves = shift_cols[:, 0:32].rearrange("p (b f t) -> p b f t", b=SAMPLES, f=2)
        scale_turns = keep.tile([P, SAMPLES, C_OUT // P], F32, name="scale_turns")
        phase_turns = keep.tile([P, SAMPLES, C_OUT // P], F32, name="phase_turns")
        nc.vector.tensor_scalar(
            out=scale_turns[:], in0=halves[:, :, 0, :], scalar1=1.0 / TWO_PI, scalar2=None, op0=ALU.mult
        )
        nc.vector.tensor_scalar(
            out=phase_turns[:],
            in0=halves[:, :, 1, :],
            scalar1=-30.0,
            scalar2=1.0 / (15.0 * TWO_PI),
            op0=ALU.add,
            op1=ALU.mult,
        )

        left_t = []
        w_codes = []
        w_scales = []
        for b in range(SAMPLES):
            left_t.append(keep.tile([P, C_OUT], BF16, name="left_t%d" % b))
            w_codes.append(keep.tile([P, PASSES, C_OUT], U32, name="w_codes%d" % b, align_bytes=64))
            w_scales.append(keep.tile([P, PASSES, C_OUT], U8, name="w_scales%d" % b, align_bytes=64))
        half_w = keep.tile([P, PASSES, C_OUT, 4], BF16, name="half_w")
        half_w_words = half_w[:].bitcast(F32)

        def transpose_left(b, step):
            bank = weight_bank([P, C_OUT // P, P], BF16)
            for t in range(C_OUT // P):
                nc.tensor.transpose(bank[:, t, :], left[b][:, t, :], ident_bf16[:])
            due(scalar_due, step + 1, lambda: nc.scalar.copy(out=left_t[b][:], in_=bank[:].rearrange("p t o -> p (t o)")))

        def halve_weight(k):
            flat = w_rows[k][:].rearrange("p t i -> p (t i)")
            nc.vector.tensor_scalar(out=flat, in0=flat, scalar1=0.5, scalar2=None, op0=ALU.mult)

        def transpose_weight(k, g, step):
            words = w_rows[k][:].bitcast(F32)
            bank = weight_bank([P, 2, PAIR], F32)
            for h in range(2):
                for t in range(2):
                    first = 256 * g + P * h
                    nc.tensor.transpose(bank[:, h, t * P : (t + 1) * P], words[:, t, first : first + P], ident_f32[:])
            due(
                scalar_due,
                step + 1,
                lambda: nc.scalar.copy(
                    out=half_w_words[:, g, PAIR * k : PAIR * (k + 1), :], in_=bank[:].rearrange("p h o -> p o h")
                ),
            )

        tanh_tiles = {}
        w_grouped = {}

        def modulate(b, g, k, t, step):
            if t == 0:
                tanh_tile = three.tile([P, PAIR, 4], F32, name="tanh_tile")
                tanh_tiles[(b, g, k)] = tanh_tile
            tanh_pair = tanh_tiles[(b, g, k)]
            first = (2 * k + t) * P
            columns = right[b][:].rearrange("r (g h p e) -> r g h e p", g=PASSES, h=2, e=2)
            bank = weight_bank([P, 4, P], F32)
            for h in range(2):
                for e in range(2):
                    nc.tensor.matmul(
                        out=bank[:, 2 * h + e, :],
                        lhsT=columns[:, g, h, e, :],
                        rhs=left_t[b][:, first : first + P],
                        start=True,
                        stop=True,
                    )
            due(
                scalar_due,
                step + 1,
                lambda: nc.scalar.activation(
                    out=tanh_pair[:, t * P : (t + 1) * P, :],
                    in_=bank[:].rearrange("p v o -> p o v"),
                    func=ACT.Tanh,
                    scale=0.5 / math.sqrt(RANK),
                ),
            )
            if t == 1:
                due(product_due, step + 1, lambda: product(b, g, k))
                due(w_quantise_due, step + 2, lambda: quantise_weight(b, g, k))

        def product(b, g, k):
            grouped = two.tile([P, PAIR, 4], BF16, name="grouped", align_bytes=64)
            nc.vector.scalar_tensor_tensor(
                out=grouped[:].rearrange("p o v -> p (o v)"),
                in0=tanh_tiles[(b, g, k)][:].rearrange("p o v -> p (o v)"),
                scalar=2.0,
                in1=half_w[:, g, PAIR * k : PAIR * (k + 1), :].rearrange("p o v -> p (o v)"),
                op0=ALU.add,
                op1=ALU.mult,
            )
            w_grouped[(b, g, k)] = grouped

        def quantise_weight(b, g, k):
            nc.vector.quantize_mx(
                out=w_codes[b][:, g, PAIR * k : PAIR * (k + 1)].bitcast(FP8X4),
                scales=w_scales[b][:, g, PAIR * k : PAIR * (k + 1)],
                in_=w_grouped[(b, g, k)][:].rearrange("p o v -> p (o v)"),
            )

        stream = []

        def add_modulation(b, k):
            for g in range(PASSES):
                for t in range(2):
                    stream.append((True, lambda step, g=g, t=t: modulate(b, g, k, t, step)))

        def add_weight(k):
            for g in range(PASSES):
                stream.append((True, lambda step, g=g: transpose_weight(k, g, step)))

        stream.append((False, lambda step: halve_weight(0)))
        stream.append((True, lambda step: transpose_left(0, step)))
        add_modulation(0, 0)
        add_weight(0)
        stream.append((False, lambda step: halve_weight(1)))
        for k in range(1, PAIRS):
            add_weight(k)
            if k + 1 < PAIRS:
                stream.append((False, lambda step, k=k: halve_weight(k + 1)))
            add_modulation(0, k)
        stream.append((True, lambda step: transpose_left(1, step)))
        for k in range(PAIRS):
            add_modulation(1, k)
        position = {"stream": 0, "x": 0}

        def halvings(step):
            while position["stream"] < len(stream) and not stream[position["stream"]][0]:
                stream[position["stream"]][1](step)
                position["stream"] += 1

        def next_weight_bank(step):
            halvings(step)
            stream[position["stream"]][1](step)
            position["stream"] += 1
            halvings(step)

        x_codes = {}
        x_scales = {}
        x_grouped = {}

        def quantise_x(c, g):
            nc.vector.quantize_mx(
                out=x_codes[c][:, g, :].bitcast(FP8X4),
                scales=x_scales[c][:, g, :],
                in_=x_grouped[(c, g)][:].rearrange("p n v -> p (n v)"),
            )

        def next_x_bank(step):
            number = position["x"]
            position["x"] += 1
            c, g, rows_half = number // 4, number // 2 % 2, number % 2
            if number % 4 == 0:
                codes = three.tile([P, PASSES, 4 * P], U32, name="codes", align_bytes=64)
                scales = three.tile([P, PASSES, 4 * P], U8, name="scales", align_bytes=64)
                x_codes[c] = codes
                x_scales[c] = scales
            if rows_half == 0:
                regrouped = four.tile([P, 4 * P, 4], BF16, name="regrouped", align_bytes=64)
                x_grouped[(c, g)] = regrouped
            words = x_rows[c][:].bitcast(F32)
            bank = psum.tile([P, 2, PAIR], F32, name="x_bank", tag="x")
            for h in range(2):
                for r in range(2):
                    first = 256 * g + P * h
                    nc.tensor.transpose(
                        bank[:, h, r * P : (r + 1) * P], words[:, 2 * rows_half + r, first : first + P], ident_f32[:]
                    )
            target = x_grouped[(c, g)][:].bitcast(F32)[:, PAIR * rows_half : PAIR * (rows_half + 1), :]
            source = bank[:].rearrange("p h n -> p n h")
            if rows_half == 0:
                due(scalar_due, step + 1, lambda: nc.scalar.copy(out=target, in_=source))
            else:
                due(copy_due, step + 1, lambda: nc.vector.tensor_copy(out=target, in_=source))
                due(x_quantise_due, step + 2, lambda: quantise_x(c, g))
            if number % 4 == 3 and c + 4 < CHUNKS:
                load_x(c + 4)

        y_banks = {}
        turns = {}
        whole = {}
        frac = {}

        def multiply(unit):
            c, k = divmod(unit, PAIRS)
            b = c // (CHUNKS // SAMPLES)
            for t in range(2):
                first = (2 * k + t) * P
                y_bank = psum.tile([P, 4 * P], F32, name="y_bank", tag="y")
                for g in range(PASSES):
                    nc.tensor.matmul_mx(
                        out=y_bank[:],
                        lhsT=w_codes[b][:, g, first : first + P].bitcast(FP8X4),
                        lhsT_scale=w_scales[b][:, g, first : first + P],
                        rhs=x_codes[c][:, g, :].bitcast(FP8X4),
                        rhs_scale=x_scales[c][:, g, :],
                        start=(g == 0),
                        stop=(g == PASSES - 1),
                    )
                y_banks[(unit, t)] = y_bank
            turns_tile = four.tile([P, 2, 4 * P], F32, name="turns_tile")
            turns[unit] = turns_tile

        def scale_and_shift(unit, on_vector):
            c, k = divmod(unit, PAIRS)
            b = c // (CHUNKS // SAMPLES)
            for t in range(2):
                tile_index = 2 * k + t
                if (unit >= VECTOR_SCALES_FROM and unit % 2 == 0 and t == 1) != on_vector:
                    continue
                if on_vector:
                    nc.vector.tensor_scalar(
                        out=turns[unit][:, t, :],
                        in0=y_banks[(unit, t)][:],
                        scalar1=scale_turns[:, b, tile_index : tile_index + 1],
                        scalar2=phase_turns[:, b, tile_index : tile_index + 1],
                        op0=ALU.mult,
                        op1=ALU.add,
                    )
                else:
                    nc.scalar.activation(
                        out=turns[unit][:, t, :],
                        in_=y_banks[(unit, t)][:],
                        func=ACT.Identity,
                        scale=scale_turns[:, b, tile_index : tile_index + 1],
                        bias=phase_turns[:, b, tile_index : tile_index + 1],
                    )

        def round_turns(unit):
            whole_tile = three.tile([P, 2, 4 * P], I32, name="whole_tile")
            nc.vector.tensor_copy(out=whole_tile[:], in_=turns[unit][:])
            whole[unit] = whole_tile

        def subtract_whole(unit):
            frac_tile = three.tile([P, 2, 4 * P], F32, name="frac_tile")
            nc.vector.tensor_tensor(out=frac_tile[:], in0=turns[unit][:], in1=whole[unit][:], op=ALU.subtract)
            frac[unit] = frac_tile

        def sine_and_store(unit):
            c, k = divmod(unit, PAIRS)
            b, q = divmod(c, CHUNKS // SAMPLES)
            t_banks = []
            for t in range(2):
                t_bank = psum.tile([P, CHUNK_R, P], F32, name="t_bank", tag="t")
                for r in range(CHUNK_R):
                    nc.tensor.transpose(t_bank[:, r, :], frac[unit][:, t, r * P : (r + 1) * P], ident_f32[:])
                t_banks.append(t_bank)
            result = three.tile([P, CHUNK_R, PAIR], F32, name="result")
            rows = out[b].rearrange("(j s) o -> j s o", s=ROWS_PP)[:, CHUNK_R * q : CHUNK_R * (q + 1), :]
            for t in range(2):
                nc.scalar.activation(out=result[:, :, t * P : (t + 1) * P], in_=t_banks[t][:], func=ACT.Sin, scale=TWO_PI)
                if unit == UNITS - 1:
                    first = PAIR * k + t * P
                    nc.sync.dma_start(out=rows[:, :, first : first + P], in_=result[:, :, t * P : (t + 1) * P])
            if unit < UNITS - 1:
                nc.sync.dma_start(out=rows[:, :, PAIR * k : PAIR * (k + 1)], in_=result[:])

        for step in range(-HEAD, UNITS + LAG_OUT):
            head_banks["on"] = step < -1
            if 0 <= step < UNITS:
                multiply(step)
            for work in scalar_due.get(step, []):
                work()
            if 0 <= step < UNITS:
                scale_and_shift(step, False)
            if 0 <= step - LAG_WHOLE < UNITS:
                round_turns(step - LAG_WHOLE)
            if 0 <= step - LAG_FRAC < UNITS:
                subtract_whole(step - LAG_FRAC)
            if 0 <= step < UNITS:
                scale_and_shift(step, True)
            for table in (copy_due, w_quantise_due, x_quantise_due, product_due):
                for work in table.get(step, []):
                    work()
            if 0 <= step - LAG_OUT < UNITS:
                sine_and_store(step - LAG_OUT)
            for turn in range(max(weight_banks(step), x_banks(step))):
                if turn < weight_banks(step):
                    next_weight_bank(step)
                if turn < x_banks(step):
                    next_x_bank(step)
